import numpy as np
import ml_dtypes


def mxq(x, axis, fmt="e4m3"):
    dtype, down = {"e4m3": (ml_dtypes.float8_e4m3fn, 7), "e5m2": (ml_dtypes.float8_e5m2, 14)}[fmt]
    v = np.moveaxis(np.asarray(x, np.float32).astype(ml_dtypes.bfloat16).astype(np.float64), axis, -1)
    blocks = v.reshape(v.shape[:-1] + (-1, 32))
    amax = np.abs(blocks).max(-1, keepdims=True)
    byte = np.maximum(np.where(amax > 0, np.frexp(amax)[1] - 1 + 127, 0) - down, 1)
    scale = np.exp2(byte - 127.0)
    codes = (blocks / scale).astype(np.float32).astype(dtype).astype(np.float64)
    return np.moveaxis((codes * scale).reshape(v.shape), -1, axis)


WIDE = False


def mx_kscale(k):
    if not WIDE:
        return np.ones(k)
    levels = np.array([10, -10, 5, -5, 0])
    a = np.random.permutation(np.resize(levels, k // 512 * 4)).reshape(k // 512, 4)
    idx = np.arange(k)
    return np.exp2(a[idx // 512, idx % 128 // 32])


BF16 = ml_dtypes.bfloat16


def bf(x):
    return np.asarray(x, np.float32).astype(BF16)


def f64(x):
    return np.asarray(x).astype(np.float64)


B, N, K, H, NUM_IN = 4, 64, 30, 512, 512


def setup_inputs():
    s, t = mx_kscale(H), mx_kscale(H)
    u = np.random.standard_normal((B, N, H))
    e = np.random.standard_normal((B, N, K, H))
    return {"h1": bf(np.maximum((u[:, :, None, :] + e) * 0.7, 0.0) * s),
            "h_V": bf(np.random.standard_normal((B, N, H))),
            "mask_attend": bf(np.random.random((B, N, K)) < 0.9),
            "W2": bf(np.random.standard_normal((H, H)) * 1.4 / np.sqrt(H) / s[:, None] * t),
            "b2": bf(np.random.standard_normal(H) * 0.2 * t),
            "W3": bf(np.random.standard_normal((H, H)) * 2.8 / np.sqrt(H) / t[:, None]),
            "b3": bf(np.random.standard_normal(H) * 0.2)}


def reference(h1, h_V, mask_attend, W2, b2, W3, b3):
    h2 = np.maximum((mxq(f64(h1), 3, "e4m3") @ mxq(f64(W2), 0, "e4m3")) + f64(b2), 0.0)
    msg = ((mxq(h2, 3, "e4m3") @ mxq(f64(W3), 0, "e4m3")) + f64(b3)) * f64(mask_attend)[..., None]
    return f64(h_V) + np.mean(msg, axis=-2)

@@ -1,0 +1,251 @@
+from contextlib import ExitStack
+
+import concourse.mybir as mybir
+from concourse.masks import make_identity
+
+F32 = mybir.dt.float32
+BF16 = mybir.dt.bfloat16
+U32 = mybir.dt.uint32
+U8 = mybir.dt.uint8
+FP8X4 = mybir.dt.float8_e4m3fn_x4
+ALU = mybir.AluOpType
+ACT = mybir.ActivationFunctionType
+
+P = 128
+PACK = 4
+HID = 512
+WORDS = HID // 2
+SLOTS = 30
+NODE_BLOCKS = 2
+SLOTS_PER_ROUND = 2
+TILES = SLOTS_PER_ROUND * NODE_BLOCKS
+COLS = TILES * P
+ROUNDS = SLOTS // SLOTS_PER_ROUND
+
+LAG_LAYER1 = 1
+LAG_REGROUP = 2
+LAG_LAYER2 = 3
+
+FLOPS = 2 * 2 * (NODE_BLOCKS * P * SLOTS) * HID * HID
+
+
+def tile_mpnnlayer_pb_kernel(tc, h1, h_V, mask_attend, W2, b2, W3, b3, out):
+    nc = tc.nc
+    h1_rows = h1.rearrange("b n k h -> (b n) (k h)")
+    hv_rows = h_V.rearrange("b n h -> (b n) h")
+    mask_rows = mask_attend.rearrange("b n k -> (b n) k")
+    out_rows = out.rearrange("b n h -> (b n) h")
+
+    with ExitStack() as ctx:
+        keep = ctx.enter_context(tc.tile_pool(name="keep", bufs=1))
+        work = ctx.enter_context(tc.tile_pool(name="work", bufs=3))
+        psum = ctx.enter_context(tc.psum_pool(name="psum", bufs=1))
+
+        h1_sb = [keep.tile([P, SLOTS * HID], BF16, name="h1_sb%d" % nb) for nb in range(NODE_BLOCKS)]
+
+        def load_h1(r):
+            cols = slice(r * SLOTS_PER_ROUND * HID, (r + 1) * SLOTS_PER_ROUND * HID)
+            for nb in range(NODE_BLOCKS):
+                nc.sync.dma_start(out=h1_sb[nb][:, cols], in_=h1_rows[nb * P : (nb + 1) * P, cols])
+
+        mask_bf = keep.tile([P, NODE_BLOCKS, SLOTS], BF16)
+        nc.sync.dma_start(out=mask_bf[:], in_=mask_rows.rearrange("(nb q) k -> q nb k", q=P))
+        load_h1(0)
+        w2_raw = keep.tile([P, PACK, HID], BF16)
+        for u in range(2):
+            nc.sync.dma_start(
+                out=w2_raw[:, 2 * u : 2 * u + 2, :],
+                in_=W2[u * 2 * P : (u + 1) * 2 * P, :].rearrange("(p e) f -> p e f", e=2),
+            )
+        b2_bf = keep.tile([P, PACK], BF16)
+        nc.sync.dma_start(out=b2_bf[:], in_=b2.rearrange("(p t) -> p t", t=PACK))
+        load_h1(1)
+        w3_raw = keep.tile([P, PACK, HID], BF16)
+        nc.sync.dma_start(out=w3_raw[:], in_=W3.rearrange("(p t) f -> p t f", t=PACK))
+        load_h1(2)
+        b3_all = keep.tile([P, HID], BF16)
+        nc.sync.dma_start(out=b3_all[:], in_=b3.partition_broadcast(P))
+        hv = keep.tile([P, NODE_BLOCKS, HID], BF16)
+        nc.sync.dma_start(out=hv[:], in_=hv_rows.rearrange("(nb q) h -> q nb h", q=P))
+        for r in range(3, ROUNDS):
+            load_h1(r)
+
+        ident = keep.tile([P, P], F32)
+        make_identity(nc, ident[:])
+        mask_f = keep.tile([P, SLOTS, NODE_BLOCKS], F32)
+        nc.vector.tensor_copy(out=mask_f[:], in_=mask_bf[:].rearrange("q nb k -> q k nb"))
+        mask_by_tile = mask_f[:].rearrange("q k nb -> q (k nb)")
+        b2_f = keep.tile([P, PACK], F32)
+        nc.vector.tensor_copy(out=b2_f[:], in_=b2_bf[:])
+
+        w2_grouped = keep.tile([P, HID, PACK], BF16, align_bytes=64)
+        nc.vector.tensor_copy(
+            out=w2_grouped[:].rearrange("p (t2 c) t -> p t2 c t", t2=PACK),
+            in_=w2_raw[:].rearrange("p t (c t2) -> p t2 c t", t2=PACK),
+        )
+        w2_codes = keep.tile([P, HID], U32, align_bytes=64)
+        w2_scales = keep.tile([P, HID], U8, align_bytes=64)
+        w3_grouped = keep.tile([P, HID, PACK], BF16, align_bytes=64)
+        nc.vector.tensor_copy(out=w3_grouped[:], in_=w3_raw[:].rearrange("p t f -> p f t"))
+        nc.vector.quantize_mx(
+            out=w2_codes[:].bitcast(FP8X4), scales=w2_scales[:], in_=w2_grouped[:].rearrange("p c t -> p (c t)")
+        )
+        w3_codes = keep.tile([P, HID], U32, align_bytes=64)
+        w3_scales = keep.tile([P, HID], U8, align_bytes=64)
+        nc.vector.quantize_mx(
+            out=w3_codes[:].bitcast(FP8X4), scales=w3_scales[:], in_=w3_grouped[:].rearrange("p f t -> p (f t)")
+        )
+
+        h1_words = [h1_sb[nb][:].bitcast(F32) for nb in range(NODE_BLOCKS)]
+        diags = {}
+        h1_q = {}
+        hiddens = {}
+        h2_q = {}
+
+        def build_diags(r):
+            diag = work.tile([P, TILES, P], F32)
+            nc.vector.tensor_tensor(
+                out=diag[:],
+                in0=ident[:].unsqueeze(1).to_broadcast([P, TILES, P]),
+                in1=mask_by_tile[:, r * TILES : (r + 1) * TILES].unsqueeze(2).to_broadcast([P, TILES, P]),
+                op=ALU.mult,
+            )
+            diags[r] = diag
+
+        def transpose_h1(r):
+            h1_grouped = work.tile([P, COLS * PACK], BF16, align_bytes=64)
+            grouped_words = h1_grouped[:].bitcast(F32).rearrange("p (c u) -> p c u", u=2)
+            for half in range(SLOTS_PER_ROUND):
+                slot = r * SLOTS_PER_ROUND + half
+                bank = psum.tile([P, 2, NODE_BLOCKS * P], F32, name="xt%d" % half)
+                for nb in range(NODE_BLOCKS):
+                    for u in range(2):
+                        first = slot * WORDS + u * P
+                        nc.tensor.transpose(
+                            bank[:, u, nb * P : (nb + 1) * P],
+                            h1_words[nb][:, first : first + P],
+                            diags[r][:, half * NODE_BLOCKS + nb, :],
+                        )
+                nc.scalar.copy(
+                    out=grouped_words[:, half * NODE_BLOCKS * P : (half + 1) * NODE_BLOCKS * P, :],
+                    in_=bank[:].rearrange("p u c -> p c u"),
+                )
+            return h1_grouped
+
+        def quantise(grouped, store):
+            codes = work.tile([P, COLS], U32, align_bytes=64, name="codes_" + store)
+            scales = work.tile([P, COLS], U8, align_bytes=64, name="scales_" + store)
+            nc.vector.quantize_mx(out=codes[:].bitcast(FP8X4), scales=scales[:], in_=grouped[:])
+            return codes, scales
+
+        def layer1(r):
+            codes, scales = h1_q[r]
+            hidden = work.tile([P, PACK, COLS], BF16)
+            for t2 in range(PACK):
+                x_ps = psum.tile([P, COLS], F32, name="x%d" % t2)
+                nc.tensor.matmul_mx(
+                    out=x_ps[:],
+                    lhsT=w2_codes[:, t2 * P : (t2 + 1) * P].bitcast(FP8X4),
+                    lhsT_scale=w2_scales[:, t2 * P : (t2 + 1) * P],
+                    rhs=codes[:].bitcast(FP8X4),
+                    rhs_scale=scales[:],
+                    start=True,
+                    stop=True,
+                )
+                nc.scalar.activation(out=hidden[:, t2, :], in_=x_ps[:], func=ACT.Relu, bias=b2_f[:, t2 : t2 + 1], scale=1.0)
+            hiddens[r] = hidden
+
+        def regroup_h2(r):
+            h2_grouped = work.tile([P, COLS * PACK], BF16, align_bytes=64)
+            nc.vector.tensor_copy(
+                out=h2_grouped[:].rearrange("p (c i t) -> p c t i", i=4, t=PACK),
+                in_=hiddens[r][:].rearrange("p t (c i) -> p c t i", i=4),
+            )
+            return h2_grouped
+
+        base = keep.tile([P, NODE_BLOCKS, HID], F32)
+
+        def idle_message_and_base():
+            idle_grouped = keep.tile([P, P, PACK], BF16, align_bytes=64)
+            nc.vector.tensor_scalar(
+                out=idle_grouped[:],
+                in0=b2_f[:].unsqueeze(1).to_broadcast([P, P, PACK]),
+                scalar1=0.0,
+                scalar2=None,
+                op0=ALU.max,
+            )
+            idle_codes = keep.tile([P, P], U32, align_bytes=64)
+            idle_scales = keep.tile([P, P], U8, align_bytes=64)
+            nc.vector.quantize_mx(
+                out=idle_codes[:].bitcast(FP8X4), scales=idle_scales[:], in_=idle_grouped[:].rearrange("p c t -> p (c t)")
+            )
+            idle_ps = psum.tile([P, HID], F32, name="acc1")
+            nc.tensor.matmul_mx(
+                out=idle_ps[:],
+                lhsT=idle_codes[:].bitcast(FP8X4),
+                lhsT_scale=idle_scales[:],
+                rhs=w3_codes[:].bitcast(FP8X4),
+                rhs_scale=w3_scales[:],
+                start=True,
+                stop=True,
+            )
+            count = keep.tile([P, NODE_BLOCKS], F32)
+            nc.vector.reduce_sum(out=count[:], in_=mask_f[:].rearrange("q k nb -> q nb k"), axis=mybir.AxisListType.X)
+            kept_share = keep.tile([P, NODE_BLOCKS], F32)
+            nc.vector.tensor_scalar(out=kept_share[:], in0=count[:], scalar1=1.0 / SLOTS, scalar2=None, op0=ALU.mult)
+            minus_masked_share = keep.tile([P, NODE_BLOCKS], F32)
+            nc.vector.tensor_scalar(
+                out=minus_masked_share[:], in0=count[:], scalar1=1.0 / SLOTS, scalar2=-1.0, op0=ALU.mult, op1=ALU.add
+            )
+            for nb in range(NODE_BLOCKS):
+                nc.vector.scalar_tensor_tensor(
+                    out=base[:, nb, :], in0=b3_all[:], scalar=kept_share[:, nb : nb + 1], in1=hv[:, nb, :],
+                    op0=ALU.mult, op1=ALU.add,
+                )
+                nc.vector.scalar_tensor_tensor(
+                    out=base[:, nb, :], in0=idle_ps[:], scalar=minus_masked_share[:, nb : nb + 1], in1=base[:, nb, :],
+                    op0=ALU.mult, op1=ALU.add,
+                )
+
+        acc = []
+
+        def layer2(r):
+            codes, scales = h2_q[r]
+            for tile_i in range(TILES):
+                slot = r * SLOTS_PER_ROUND + tile_i // NODE_BLOCKS
+                nc.tensor.matmul_mx(
+                    out=acc[tile_i % NODE_BLOCKS][:],
+                    lhsT=codes[:, tile_i * P : (tile_i + 1) * P].bitcast(FP8X4),
+                    lhsT_scale=scales[:, tile_i * P : (tile_i + 1) * P],
+                    rhs=w3_codes[:].bitcast(FP8X4),
+                    rhs_scale=w3_scales[:],
+                    start=(slot == 0),
+                    stop=(slot == SLOTS - 1),
+                )
+
+        build_diags(0)
+        for step in range(ROUNDS + LAG_LAYER2):
+            if step < ROUNDS:
+                h1_grouped = transpose_h1(step)
+            if 0 <= step - LAG_LAYER1 < ROUNDS:
+                layer1(step - LAG_LAYER1)
+            if 0 <= step - LAG_REGROUP < ROUNDS:
+                h2_grouped = regroup_h2(step - LAG_REGROUP)
+            if step < ROUNDS:
+                h1_q[step] = quantise(h1_grouped, "h1")
+            if 0 <= step - LAG_REGROUP < ROUNDS:
+                h2_q[step - LAG_REGROUP] = quantise(h2_grouped, "h2")
+            if step + 1 < ROUNDS:
+                build_diags(step + 1)
+            if step == LAG_LAYER2:
+                idle_message_and_base()
+                acc.extend([psum.tile([P, HID], F32, name="acc%d" % nb) for nb in range(NODE_BLOCKS)])
+            if step >= LAG_LAYER2:
+                layer2(step - LAG_LAYER2)
+
+        result = keep.tile([P, NODE_BLOCKS, HID], F32)
+        for nb in range(NODE_BLOCKS):
+            nc.vector.scalar_tensor_tensor(
+                out=result[:, nb, :], in0=acc[nb][:], scalar=1.0 / SLOTS, in1=base[:, nb, :], op0=ALU.mult, op1=ALU.add
+            )
+            nc.sync.dma_start(out=out_rows[nb * P : (nb + 1) * P, :], in_=result[:, nb, :])

@@ -18,13 +18,14 @@ WORDS = HID // 2
 SLOTS = 30
 NODE_BLOCKS = 2
 SLOTS_PER_ROUND = 2
-TILES = SLOTS_PER_ROUND * NODE_BLOCKS
+TILES = NODE_BLOCKS * SLOTS_PER_ROUND
 COLS = TILES * P
 ROUNDS = SLOTS // SLOTS_PER_ROUND
 
 LAG_LAYER1 = 1
 LAG_REGROUP = 2
 LAG_LAYER2 = 3
+STEP_OF_W3 = 1
 
 FLOPS = 2 * 2 * (NODE_BLOCKS * P * SLOTS) * HID * HID
 
@@ -38,7 +39,7 @@ def tile_mpnnlayer_pb_kernel(tc, h1, h_V, mask_attend, W2, b2, W3, b3, out):
 
     with ExitStack() as ctx:
         keep = ctx.enter_context(tc.tile_pool(name="keep", bufs=1))
-        work = ctx.enter_context(tc.tile_pool(name="work", bufs=3))
+        work = ctx.enter_context(tc.tile_pool(name="work", bufs=4))
         psum = ctx.enter_context(tc.psum_pool(name="psum", bufs=1))
 
         h1_sb = [keep.tile([P, SLOTS * HID], BF16, name="h1_sb%d" % nb) for nb in range(NODE_BLOCKS)]
@@ -72,12 +73,21 @@ def tile_mpnnlayer_pb_kernel(tc, h1, h_V, mask_attend, W2, b2, W3, b3, out):
 
         ident = keep.tile([P, P], F32)
         make_identity(nc, ident[:])
-        mask_f = keep.tile([P, SLOTS, NODE_BLOCKS], F32)
-        nc.vector.tensor_copy(out=mask_f[:], in_=mask_bf[:].rearrange("q nb k -> q k nb"))
-        mask_by_tile = mask_f[:].rearrange("q k nb -> q (k nb)")
+        mask_f = keep.tile([P, ROUNDS, NODE_BLOCKS, SLOTS_PER_ROUND], F32)
+        nc.gpsimd.tensor_copy(out=mask_f[:], in_=mask_bf[:].rearrange("q nb (r s) -> q r nb s", s=SLOTS_PER_ROUND))
+        diags = []
+        for r in range(ROUNDS):
+            diag = keep.tile([P, TILES, P], F32, name="diag%d" % r)
+            nc.gpsimd.tensor_tensor(
+                out=diag[:],
+                in0=ident[:].unsqueeze(1).to_broadcast([P, TILES, P]),
+                in1=mask_f[:, r, :, :].rearrange("q nb s -> q (nb s)").unsqueeze(2).to_broadcast([P, TILES, P]),
+                op=ALU.mult,
+            )
+            diags.append(diag)
+
         b2_f = keep.tile([P, PACK], F32)
         nc.vector.tensor_copy(out=b2_f[:], in_=b2_bf[:])
-
         w2_grouped = keep.tile([P, HID, PACK], BF16, align_bytes=64)
         nc.vector.tensor_copy(
             out=w2_grouped[:].rearrange("p (t2 c) t -> p t2 c t", t2=PACK),
@@ -85,49 +95,30 @@ def tile_mpnnlayer_pb_kernel(tc, h1, h_V, mask_attend, W2, b2, W3, b3, out):
         )
         w2_codes = keep.tile([P, HID], U32, align_bytes=64)
         w2_scales = keep.tile([P, HID], U8, align_bytes=64)
-        w3_grouped = keep.tile([P, HID, PACK], BF16, align_bytes=64)
-        nc.vector.tensor_copy(out=w3_grouped[:], in_=w3_raw[:].rearrange("p t f -> p f t"))
         nc.vector.quantize_mx(
             out=w2_codes[:].bitcast(FP8X4), scales=w2_scales[:], in_=w2_grouped[:].rearrange("p c t -> p (c t)")
         )
-        w3_codes = keep.tile([P, HID], U32, align_bytes=64)
-        w3_scales = keep.tile([P, HID], U8, align_bytes=64)
-        nc.vector.quantize_mx(
-            out=w3_codes[:].bitcast(FP8X4), scales=w3_scales[:], in_=w3_grouped[:].rearrange("p f t -> p (f t)")
-        )
 
         h1_words = [h1_sb[nb][:].bitcast(F32) for nb in range(NODE_BLOCKS)]
-        diags = {}
         h1_q = {}
         hiddens = {}
         h2_q = {}
 
-        def build_diags(r):
-            diag = work.tile([P, TILES, P], F32)
-            nc.vector.tensor_tensor(
-                out=diag[:],
-                in0=ident[:].unsqueeze(1).to_broadcast([P, TILES, P]),
-                in1=mask_by_tile[:, r * TILES : (r + 1) * TILES].unsqueeze(2).to_broadcast([P, TILES, P]),
-                op=ALU.mult,
-            )
-            diags[r] = diag
-
         def transpose_h1(r):
             h1_grouped = work.tile([P, COLS * PACK], BF16, align_bytes=64)
             grouped_words = h1_grouped[:].bitcast(F32).rearrange("p (c u) -> p c u", u=2)
-            for half in range(SLOTS_PER_ROUND):
-                slot = r * SLOTS_PER_ROUND + half
-                bank = psum.tile([P, 2, NODE_BLOCKS * P], F32, name="xt%d" % half)
-                for nb in range(NODE_BLOCKS):
+            for nb in range(NODE_BLOCKS):
+                bank = psum.tile([P, 2, SLOTS_PER_ROUND * P], F32, name="xt%d" % nb)
+                for s in range(SLOTS_PER_ROUND):
                     for u in range(2):
-                        first = slot * WORDS + u * P
+                        first = (r * SLOTS_PER_ROUND + s) * WORDS + u * P
                         nc.tensor.transpose(
-                            bank[:, u, nb * P : (nb + 1) * P],
+                            bank[:, u, s * P : (s + 1) * P],
                             h1_words[nb][:, first : first + P],
-                            diags[r][:, half * NODE_BLOCKS + nb, :],
+                            diags[r][:, nb * SLOTS_PER_ROUND + s, :],
                         )
                 nc.scalar.copy(
-                    out=grouped_words[:, half * NODE_BLOCKS * P : (half + 1) * NODE_BLOCKS * P, :],
+                    out=grouped_words[:, nb * SLOTS_PER_ROUND * P : (nb + 1) * SLOTS_PER_ROUND * P, :],
                     in_=bank[:].rearrange("p u c -> p c u"),
                 )
             return h1_grouped
@@ -152,7 +143,15 @@ def tile_mpnnlayer_pb_kernel(tc, h1, h_V, mask_attend, W2, b2, W3, b3, out):
                     start=True,
                     stop=True,
                 )
-                nc.scalar.activation(out=hidden[:, t2, :], in_=x_ps[:], func=ACT.Relu, bias=b2_f[:, t2 : t2 + 1], scale=1.0)
+                if t2 < PACK - 1:
+                    nc.scalar.activation(
+                        out=hidden[:, t2, :], in_=x_ps[:], func=ACT.Relu, bias=b2_f[:, t2 : t2 + 1], scale=1.0
+                    )
+                else:
+                    nc.vector.tensor_scalar(
+                        out=hidden[:, t2, :], in0=x_ps[:], scalar1=b2_f[:, t2 : t2 + 1], scalar2=0.0,
+                        op0=ALU.add, op1=ALU.max,
+                    )
             hiddens[r] = hidden
 
         def regroup_h2(r):
@@ -163,9 +162,13 @@ def tile_mpnnlayer_pb_kernel(tc, h1, h_V, mask_attend, W2, b2, W3, b3, out):
             )
             return h2_grouped
 
+        w3_codes = keep.tile([P, HID], U32, align_bytes=64)
+        w3_scales = keep.tile([P, HID], U8, align_bytes=64)
         base = keep.tile([P, NODE_BLOCKS, HID], F32)
 
-        def idle_message_and_base():
+        def prepare_w3_and_base():
+            w3_grouped = keep.tile([P, HID, PACK], BF16, align_bytes=64)
+            nc.vector.tensor_copy(out=w3_grouped[:], in_=w3_raw[:].rearrange("p t f -> p f t"))
             idle_grouped = keep.tile([P, P, PACK], BF16, align_bytes=64)
             nc.vector.tensor_scalar(
                 out=idle_grouped[:],
@@ -173,6 +176,9 @@ def tile_mpnnlayer_pb_kernel(tc, h1, h_V, mask_attend, W2, b2, W3, b3, out):
                 scalar1=0.0,
                 scalar2=None,
                 op0=ALU.max,
+            )
+            nc.vector.quantize_mx(
+                out=w3_codes[:].bitcast(FP8X4), scales=w3_scales[:], in_=w3_grouped[:].rearrange("p f t -> p (f t)")
             )
             idle_codes = keep.tile([P, P], U32, align_bytes=64)
             idle_scales = keep.tile([P, P], U8, align_bytes=64)
@@ -190,7 +196,7 @@ def tile_mpnnlayer_pb_kernel(tc, h1, h_V, mask_attend, W2, b2, W3, b3, out):
                 stop=True,
             )
             count = keep.tile([P, NODE_BLOCKS], F32)
-            nc.vector.reduce_sum(out=count[:], in_=mask_f[:].rearrange("q k nb -> q nb k"), axis=mybir.AxisListType.X)
+            nc.vector.reduce_sum(out=count[:], in_=mask_f[:].rearrange("q r nb s -> q nb r s"), axis=mybir.AxisListType.XY)
             kept_share = keep.tile([P, NODE_BLOCKS], F32)
             nc.vector.tensor_scalar(out=kept_share[:], in0=count[:], scalar1=1.0 / SLOTS, scalar2=None, op0=ALU.mult)
             minus_masked_share = keep.tile([P, NODE_BLOCKS], F32)
@@ -211,34 +217,33 @@ def tile_mpnnlayer_pb_kernel(tc, h1, h_V, mask_attend, W2, b2, W3, b3, out):
 
         def layer2(r):
             codes, scales = h2_q[r]
-            for tile_i in range(TILES):
-                slot = r * SLOTS_PER_ROUND + tile_i // NODE_BLOCKS
-                nc.tensor.matmul_mx(
-                    out=acc[tile_i % NODE_BLOCKS][:],
-                    lhsT=codes[:, tile_i * P : (tile_i + 1) * P].bitcast(FP8X4),
-                    lhsT_scale=scales[:, tile_i * P : (tile_i + 1) * P],
-                    rhs=w3_codes[:].bitcast(FP8X4),
-                    rhs_scale=w3_scales[:],
-                    start=(slot == 0),
-                    stop=(slot == SLOTS - 1),
-                )
+            for nb in range(NODE_BLOCKS):
+                for s in range(SLOTS_PER_ROUND):
+                    cols = slice((nb * SLOTS_PER_ROUND + s) * P, (nb * SLOTS_PER_ROUND + s + 1) * P)
+                    slot = r * SLOTS_PER_ROUND + s
+                    nc.tensor.matmul_mx(
+                        out=acc[nb][:],
+                        lhsT=codes[:, cols].bitcast(FP8X4),
+                        lhsT_scale=scales[:, cols],
+                        rhs=w3_codes[:].bitcast(FP8X4),
+                        rhs_scale=w3_scales[:],
+                        start=(slot == 0),
+                        stop=(slot == SLOTS - 1),
+                    )
 
-        build_diags(0)
         for step in range(ROUNDS + LAG_LAYER2):
             if step < ROUNDS:
                 h1_grouped = transpose_h1(step)
-            if 0 <= step - LAG_LAYER1 < ROUNDS:
-                layer1(step - LAG_LAYER1)
             if 0 <= step - LAG_REGROUP < ROUNDS:
                 h2_grouped = regroup_h2(step - LAG_REGROUP)
             if step < ROUNDS:
                 h1_q[step] = quantise(h1_grouped, "h1")
             if 0 <= step - LAG_REGROUP < ROUNDS:
                 h2_q[step - LAG_REGROUP] = quantise(h2_grouped, "h2")
-            if step + 1 < ROUNDS:
-                build_diags(step + 1)
-            if step == LAG_LAYER2:
-                idle_message_and_base()
+            if 0 <= step - LAG_LAYER1 < ROUNDS:
+                layer1(step - LAG_LAYER1)
+            if step == STEP_OF_W3:
+                prepare_w3_and_base()
                 acc.extend([psum.tile([P, HID], F32, name="acc%d" % nb) for nb in range(NODE_BLOCKS)])
             if step >= LAG_LAYER2:
                 layer2(step - LAG_LAYER2)

@@ -23,9 +23,9 @@ COLS = TILES * P
 ROUNDS = SLOTS // SLOTS_PER_ROUND
 
 LAG_LAYER1 = 1
-LAG_REGROUP = 2
-LAG_LAYER2 = 3
-STEP_OF_W3 = 1
+LAG_LAYER2 = 2
+STEP_OF_W3 = 0
+STEP_OF_BASE = ROUNDS - 1
 
 FLOPS = 2 * 2 * (NODE_BLOCKS * P * SLOTS) * HID * HID
 
@@ -38,8 +38,9 @@ def tile_mpnnlayer_pb_kernel(tc, h1, h_V, mask_attend, W2, b2, W3, b3, out):
     out_rows = out.rearrange("b n h -> (b n) h")
 
     with ExitStack() as ctx:
+        ctx.enter_context(tc.manual_schedule())
         keep = ctx.enter_context(tc.tile_pool(name="keep", bufs=1))
-        work = ctx.enter_context(tc.tile_pool(name="work", bufs=4))
+        work = ctx.enter_context(tc.tile_pool(name="work", bufs=3))
         psum = ctx.enter_context(tc.psum_pool(name="psum", bufs=1))
 
         h1_sb = [keep.tile([P, SLOTS * HID], BF16, name="h1_sb%d" % nb) for nb in range(NODE_BLOCKS)]
@@ -63,50 +64,35 @@ def tile_mpnnlayer_pb_kernel(tc, h1, h_V, mask_attend, W2, b2, W3, b3, out):
         load_h1(1)
         w3_raw = keep.tile([P, PACK, HID], BF16)
         nc.sync.dma_start(out=w3_raw[:], in_=W3.rearrange("(p t) f -> p t f", t=PACK))
-        load_h1(2)
+        for r in range(2, ROUNDS):
+            load_h1(r)
         b3_all = keep.tile([P, HID], BF16)
         nc.sync.dma_start(out=b3_all[:], in_=b3.partition_broadcast(P))
         hv = keep.tile([P, NODE_BLOCKS, HID], BF16)
         nc.sync.dma_start(out=hv[:], in_=hv_rows.rearrange("(nb q) h -> q nb h", q=P))
-        for r in range(3, ROUNDS):
-            load_h1(r)
 
         ident = keep.tile([P, P], F32)
         make_identity(nc, ident[:])
         mask_f = keep.tile([P, ROUNDS, NODE_BLOCKS, SLOTS_PER_ROUND], F32)
-        nc.gpsimd.tensor_copy(out=mask_f[:], in_=mask_bf[:].rearrange("q nb (r s) -> q r nb s", s=SLOTS_PER_ROUND))
-        diags = []
-        for r in range(ROUNDS):
-            diag = keep.tile([P, TILES, P], F32, name="diag%d" % r)
-            nc.gpsimd.tensor_tensor(
+        nc.vector.tensor_copy(out=mask_f[:], in_=mask_bf[:].rearrange("q nb (r s) -> q r nb s", s=SLOTS_PER_ROUND))
+        h1_words = [h1_sb[nb][:].bitcast(F32) for nb in range(NODE_BLOCKS)]
+        diags = {}
+        banks = {}
+        h1_q = {}
+        hiddens = {}
+
+        def build_diags(r):
+            diag = work.tile([P, TILES, P], F32)
+            nc.vector.tensor_tensor(
                 out=diag[:],
                 in0=ident[:].unsqueeze(1).to_broadcast([P, TILES, P]),
                 in1=mask_f[:, r, :, :].rearrange("q nb s -> q (nb s)").unsqueeze(2).to_broadcast([P, TILES, P]),
                 op=ALU.mult,
             )
-            diags.append(diag)
-
-        b2_f = keep.tile([P, PACK], F32)
-        nc.vector.tensor_copy(out=b2_f[:], in_=b2_bf[:])
-        w2_grouped = keep.tile([P, HID, PACK], BF16, align_bytes=64)
-        nc.vector.tensor_copy(
-            out=w2_grouped[:].rearrange("p (t2 c) t -> p t2 c t", t2=PACK),
-            in_=w2_raw[:].rearrange("p t (c t2) -> p t2 c t", t2=PACK),
-        )
-        w2_codes = keep.tile([P, HID], U32, align_bytes=64)
-        w2_scales = keep.tile([P, HID], U8, align_bytes=64)
-        nc.vector.quantize_mx(
-            out=w2_codes[:].bitcast(FP8X4), scales=w2_scales[:], in_=w2_grouped[:].rearrange("p c t -> p (c t)")
-        )
-
-        h1_words = [h1_sb[nb][:].bitcast(F32) for nb in range(NODE_BLOCKS)]
-        h1_q = {}
-        hiddens = {}
-        h2_q = {}
+            diags[r] = diag
 
         def transpose_h1(r):
-            h1_grouped = work.tile([P, COLS * PACK], BF16, align_bytes=64)
-            grouped_words = h1_grouped[:].bitcast(F32).rearrange("p (c u) -> p c u", u=2)
+            banks[r] = []
             for nb in range(NODE_BLOCKS):
                 bank = psum.tile([P, 2, SLOTS_PER_ROUND * P], F32, name="xt%d" % nb)
                 for s in range(SLOTS_PER_ROUND):
@@ -117,9 +103,15 @@ def tile_mpnnlayer_pb_kernel(tc, h1, h_V, mask_attend, W2, b2, W3, b3, out):
                             h1_words[nb][:, first : first + P],
                             diags[r][:, nb * SLOTS_PER_ROUND + s, :],
                         )
+                banks[r].append(bank)
+
+        def group_h1(r):
+            h1_grouped = work.tile([P, COLS * PACK], BF16, align_bytes=64)
+            grouped_words = h1_grouped[:].bitcast(F32).rearrange("p (c u) -> p c u", u=2)
+            for nb in range(NODE_BLOCKS):
                 nc.scalar.copy(
                     out=grouped_words[:, nb * SLOTS_PER_ROUND * P : (nb + 1) * SLOTS_PER_ROUND * P, :],
-                    in_=bank[:].rearrange("p u c -> p c u"),
+                    in_=banks[r][nb][:].rearrange("p u c -> p c u"),
                 )
             return h1_grouped
 
@@ -128,6 +120,21 @@ def tile_mpnnlayer_pb_kernel(tc, h1, h_V, mask_attend, W2, b2, W3, b3, out):
             scales = work.tile([P, COLS], U8, align_bytes=64, name="scales_" + store)
             nc.vector.quantize_mx(out=codes[:].bitcast(FP8X4), scales=scales[:], in_=grouped[:])
             return codes, scales
+
+        w2_codes = keep.tile([P, HID], U32, align_bytes=64)
+        w2_scales = keep.tile([P, HID], U8, align_bytes=64)
+        b2_f = keep.tile([P, PACK], F32)
+
+        def prepare_w2():
+            nc.vector.tensor_copy(out=b2_f[:], in_=b2_bf[:])
+            w2_grouped = keep.tile([P, HID, PACK], BF16, align_bytes=64)
+            nc.vector.tensor_copy(
+                out=w2_grouped[:].rearrange("p (t2 c) t -> p t2 c t", t2=PACK),
+                in_=w2_raw[:].rearrange("p t (c t2) -> p t2 c t", t2=PACK),
+            )
+            nc.vector.quantize_mx(
+                out=w2_codes[:].bitcast(FP8X4), scales=w2_scales[:], in_=w2_grouped[:].rearrange("p c t -> p (c t)")
+            )
 
         def layer1(r):
             codes, scales = h1_q[r]
@@ -143,15 +150,7 @@ def tile_mpnnlayer_pb_kernel(tc, h1, h_V, mask_attend, W2, b2, W3, b3, out):
                     start=True,
                     stop=True,
                 )
-                if t2 < PACK - 1:
-                    nc.scalar.activation(
-                        out=hidden[:, t2, :], in_=x_ps[:], func=ACT.Relu, bias=b2_f[:, t2 : t2 + 1], scale=1.0
-                    )
-                else:
-                    nc.vector.tensor_scalar(
-                        out=hidden[:, t2, :], in0=x_ps[:], scalar1=b2_f[:, t2 : t2 + 1], scalar2=0.0,
-                        op0=ALU.add, op1=ALU.max,
-                    )
+                nc.scalar.activation(out=hidden[:, t2, :], in_=x_ps[:], func=ACT.Relu, bias=b2_f[:, t2 : t2 + 1], scale=1.0)
             hiddens[r] = hidden
 
         def regroup_h2(r):
@@ -164,11 +163,17 @@ def tile_mpnnlayer_pb_kernel(tc, h1, h_V, mask_attend, W2, b2, W3, b3, out):
 
         w3_codes = keep.tile([P, HID], U32, align_bytes=64)
         w3_scales = keep.tile([P, HID], U8, align_bytes=64)
-        base = keep.tile([P, NODE_BLOCKS, HID], F32)
 
-        def prepare_w3_and_base():
+        def prepare_w3():
             w3_grouped = keep.tile([P, HID, PACK], BF16, align_bytes=64)
             nc.vector.tensor_copy(out=w3_grouped[:], in_=w3_raw[:].rearrange("p t f -> p f t"))
+            nc.vector.quantize_mx(
+                out=w3_codes[:].bitcast(FP8X4), scales=w3_scales[:], in_=w3_grouped[:].rearrange("p f t -> p (f t)")
+            )
+
+        base = keep.tile([P, NODE_BLOCKS, HID], F32)
+
+        def prepare_base():
             idle_grouped = keep.tile([P, P, PACK], BF16, align_bytes=64)
             nc.vector.tensor_scalar(
                 out=idle_grouped[:],
@@ -177,15 +182,14 @@ def tile_mpnnlayer_pb_kernel(tc, h1, h_V, mask_attend, W2, b2, W3, b3, out):
                 scalar2=None,
                 op0=ALU.max,
             )
-            nc.vector.quantize_mx(
-                out=w3_codes[:].bitcast(FP8X4), scales=w3_scales[:], in_=w3_grouped[:].rearrange("p f t -> p (f t)")
-            )
+            count = keep.tile([P, NODE_BLOCKS], F32)
+            nc.vector.reduce_sum(out=count[:], in_=mask_f[:].rearrange("q r nb s -> q nb r s"), axis=mybir.AxisListType.XY)
             idle_codes = keep.tile([P, P], U32, align_bytes=64)
             idle_scales = keep.tile([P, P], U8, align_bytes=64)
             nc.vector.quantize_mx(
                 out=idle_codes[:].bitcast(FP8X4), scales=idle_scales[:], in_=idle_grouped[:].rearrange("p c t -> p (c t)")
             )
-            idle_ps = psum.tile([P, HID], F32, name="acc1")
+            idle_ps = psum.tile([P, HID], F32, name="xt0")
             nc.tensor.matmul_mx(
                 out=idle_ps[:],
                 lhsT=idle_codes[:].bitcast(FP8X4),
@@ -195,8 +199,6 @@ def tile_mpnnlayer_pb_kernel(tc, h1, h_V, mask_attend, W2, b2, W3, b3, out):
                 start=True,
                 stop=True,
             )
-            count = keep.tile([P, NODE_BLOCKS], F32)
-            nc.vector.reduce_sum(out=count[:], in_=mask_f[:].rearrange("q r nb s -> q nb r s"), axis=mybir.AxisListType.XY)
             kept_share = keep.tile([P, NODE_BLOCKS], F32)
             nc.vector.tensor_scalar(out=kept_share[:], in0=count[:], scalar1=1.0 / SLOTS, scalar2=None, op0=ALU.mult)
             minus_masked_share = keep.tile([P, NODE_BLOCKS], F32)
@@ -208,15 +210,15 @@ def tile_mpnnlayer_pb_kernel(tc, h1, h_V, mask_attend, W2, b2, W3, b3, out):
                     out=base[:, nb, :], in0=b3_all[:], scalar=kept_share[:, nb : nb + 1], in1=hv[:, nb, :],
                     op0=ALU.mult, op1=ALU.add,
                 )
+            for nb in range(NODE_BLOCKS):
                 nc.vector.scalar_tensor_tensor(
                     out=base[:, nb, :], in0=idle_ps[:], scalar=minus_masked_share[:, nb : nb + 1], in1=base[:, nb, :],
                     op0=ALU.mult, op1=ALU.add,
                 )
 
-        acc = []
+        acc = [psum.tile([P, HID], F32, name="acc%d" % nb) for nb in range(NODE_BLOCKS)]
 
-        def layer2(r):
-            codes, scales = h2_q[r]
+        def layer2(r, codes, scales):
             for nb in range(NODE_BLOCKS):
                 for s in range(SLOTS_PER_ROUND):
                     cols = slice((nb * SLOTS_PER_ROUND + s) * P, (nb * SLOTS_PER_ROUND + s + 1) * P)
@@ -231,22 +233,30 @@ def tile_mpnnlayer_pb_kernel(tc, h1, h_V, mask_attend, W2, b2, W3, b3, out):
                         stop=(slot == SLOTS - 1),
                     )
 
+        build_diags(0)
+        build_diags(1)
+        transpose_h1(0)
+        prepare_w2()
         for step in range(ROUNDS + LAG_LAYER2):
             if step < ROUNDS:
-                h1_grouped = transpose_h1(step)
-            if 0 <= step - LAG_REGROUP < ROUNDS:
-                h2_grouped = regroup_h2(step - LAG_REGROUP)
-            if step < ROUNDS:
-                h1_q[step] = quantise(h1_grouped, "h1")
-            if 0 <= step - LAG_REGROUP < ROUNDS:
-                h2_q[step - LAG_REGROUP] = quantise(h2_grouped, "h2")
+                h1_grouped = group_h1(step)
+            if step >= LAG_LAYER2:
+                h2_grouped = regroup_h2(step - LAG_LAYER2)
             if 0 <= step - LAG_LAYER1 < ROUNDS:
                 layer1(step - LAG_LAYER1)
-            if step == STEP_OF_W3:
-                prepare_w3_and_base()
-                acc.extend([psum.tile([P, HID], F32, name="acc%d" % nb) for nb in range(NODE_BLOCKS)])
+            if step < ROUNDS:
+                h1_q[step] = quantise(h1_grouped, "h1")
+            if step + 1 < ROUNDS:
+                transpose_h1(step + 1)
             if step >= LAG_LAYER2:
-                layer2(step - LAG_LAYER2)
+                h2_codes, h2_scales = quantise(h2_grouped, "h2")
+                layer2(step - LAG_LAYER2, h2_codes, h2_scales)
+            if step + 2 < ROUNDS:
+                build_diags(step + 2)
+            if step == STEP_OF_W3:
+                prepare_w3()
+            if step == STEP_OF_BASE:
+                prepare_base()
 
         result = keep.tile([P, NODE_BLOCKS, HID], F32)
         for nb in range(NODE_BLOCKS):

@@ -23,9 +23,11 @@ COLS = TILES * P
 ROUNDS = SLOTS // SLOTS_PER_ROUND
 
 LAG_LAYER1 = 1
-LAG_LAYER2 = 2
+LAG_REGROUP = 2
+LAG_LAYER2 = 3
 STEP_OF_W3 = 0
 STEP_OF_BASE = ROUNDS - 1
+LAST_ROUND_PIECES = NODE_BLOCKS
 
 FLOPS = 2 * 2 * (NODE_BLOCKS * P * SLOTS) * HID * HID
 
@@ -52,7 +54,6 @@ def tile_mpnnlayer_pb_kernel(tc, h1, h_V, mask_attend, W2, b2, W3, b3, out):
 
         mask_bf = keep.tile([P, NODE_BLOCKS, SLOTS], BF16)
         nc.sync.dma_start(out=mask_bf[:], in_=mask_rows.rearrange("(nb q) k -> q nb k", q=P))
-        load_h1(0)
         w2_raw = keep.tile([P, PACK, HID], BF16)
         for u in range(2):
             nc.sync.dma_start(
@@ -61,6 +62,7 @@ def tile_mpnnlayer_pb_kernel(tc, h1, h_V, mask_attend, W2, b2, W3, b3, out):
             )
         b2_bf = keep.tile([P, PACK], BF16)
         nc.sync.dma_start(out=b2_bf[:], in_=b2.rearrange("(p t) -> p t", t=PACK))
+        load_h1(0)
         load_h1(1)
         w3_raw = keep.tile([P, PACK, HID], BF16)
         nc.sync.dma_start(out=w3_raw[:], in_=W3.rearrange("(p t) f -> p t f", t=PACK))
@@ -80,6 +82,7 @@ def tile_mpnnlayer_pb_kernel(tc, h1, h_V, mask_attend, W2, b2, W3, b3, out):
         banks = {}
         h1_q = {}
         hiddens = {}
+        h2_q = {}
 
         def build_diags(r):
             diag = work.tile([P, TILES, P], F32)
@@ -115,11 +118,18 @@ def tile_mpnnlayer_pb_kernel(tc, h1, h_V, mask_attend, W2, b2, W3, b3, out):
                 )
             return h1_grouped
 
-        def quantise(grouped, store):
-            codes = work.tile([P, COLS], U32, align_bytes=64, name="codes_" + store)
-            scales = work.tile([P, COLS], U8, align_bytes=64, name="scales_" + store)
-            nc.vector.quantize_mx(out=codes[:].bitcast(FP8X4), scales=scales[:], in_=grouped[:])
-            return codes, scales
+        def quantise_h1(r, h1_grouped):
+            h1_codes = work.tile([P, COLS], U32, align_bytes=64)
+            h1_scales = work.tile([P, COLS], U8, align_bytes=64)
+            nc.vector.quantize_mx(out=h1_codes[:].bitcast(FP8X4), scales=h1_scales[:], in_=h1_grouped[:])
+            h1_q[r] = (h1_codes, h1_scales)
+
+        def pieces_of(r):
+            return LAST_ROUND_PIECES if r == ROUNDS - 1 else 1
+
+        def piece_cols(r, piece):
+            width = COLS // pieces_of(r)
+            return slice(piece * width, (piece + 1) * width)
 
         w2_codes = keep.tile([P, HID], U32, align_bytes=64)
         w2_scales = keep.tile([P, HID], U8, align_bytes=64)
@@ -139,27 +149,30 @@ def tile_mpnnlayer_pb_kernel(tc, h1, h_V, mask_attend, W2, b2, W3, b3, out):
         def layer1(r):
             codes, scales = h1_q[r]
             hidden = work.tile([P, PACK, COLS], BF16)
-            for t2 in range(PACK):
-                x_ps = psum.tile([P, COLS], F32, name="x%d" % t2)
-                nc.tensor.matmul_mx(
-                    out=x_ps[:],
-                    lhsT=w2_codes[:, t2 * P : (t2 + 1) * P].bitcast(FP8X4),
-                    lhsT_scale=w2_scales[:, t2 * P : (t2 + 1) * P],
-                    rhs=codes[:].bitcast(FP8X4),
-                    rhs_scale=scales[:],
-                    start=True,
-                    stop=True,
-                )
-                nc.scalar.activation(out=hidden[:, t2, :], in_=x_ps[:], func=ACT.Relu, bias=b2_f[:, t2 : t2 + 1], scale=1.0)
+            x_banks = [psum.tile([P, COLS], F32, name="x%d" % t2) for t2 in range(PACK)]
+            for piece in range(pieces_of(r)):
+                cols = piece_cols(r, piece)
+                for t2 in range(PACK):
+                    nc.tensor.matmul_mx(
+                        out=x_banks[t2][:, cols],
+                        lhsT=w2_codes[:, t2 * P : (t2 + 1) * P].bitcast(FP8X4),
+                        lhsT_scale=w2_scales[:, t2 * P : (t2 + 1) * P],
+                        rhs=codes[:, cols].bitcast(FP8X4),
+                        rhs_scale=scales[:, cols],
+                        start=True,
+                        stop=True,
+                    )
+                    nc.scalar.activation(
+                        out=hidden[:, t2, cols], in_=x_banks[t2][:, cols], func=ACT.Relu, bias=b2_f[:, t2 : t2 + 1], scale=1.0
+                    )
             hiddens[r] = hidden
 
-        def regroup_h2(r):
-            h2_grouped = work.tile([P, COLS * PACK], BF16, align_bytes=64)
+        def regroup_h2(r, h2_grouped, piece):
+            cols = piece_cols(r, piece)
             nc.vector.tensor_copy(
-                out=h2_grouped[:].rearrange("p (c i t) -> p c t i", i=4, t=PACK),
-                in_=hiddens[r][:].rearrange("p t (c i) -> p c t i", i=4),
+                out=h2_grouped[:, cols, :].rearrange("p (c i) t -> p c t i", i=4),
+                in_=hiddens[r][:, :, cols].rearrange("p t (c i) -> p c t i", i=4),
             )
-            return h2_grouped
 
         w3_codes = keep.tile([P, HID], U32, align_bytes=64)
         w3_scales = keep.tile([P, HID], U8, align_bytes=64)
@@ -218,39 +231,54 @@ def tile_mpnnlayer_pb_kernel(tc, h1, h_V, mask_attend, W2, b2, W3, b3, out):
 
         acc = [psum.tile([P, HID], F32, name="acc%d" % nb) for nb in range(NODE_BLOCKS)]
 
-        def layer2(r, codes, scales):
-            for nb in range(NODE_BLOCKS):
-                for s in range(SLOTS_PER_ROUND):
-                    cols = slice((nb * SLOTS_PER_ROUND + s) * P, (nb * SLOTS_PER_ROUND + s + 1) * P)
-                    slot = r * SLOTS_PER_ROUND + s
-                    nc.tensor.matmul_mx(
-                        out=acc[nb][:],
-                        lhsT=codes[:, cols].bitcast(FP8X4),
-                        lhsT_scale=scales[:, cols],
-                        rhs=w3_codes[:].bitcast(FP8X4),
-                        rhs_scale=w3_scales[:],
-                        start=(slot == 0),
-                        stop=(slot == SLOTS - 1),
-                    )
+        def quantise_h2(r, h2_grouped):
+            h2_codes = work.tile([P, COLS], U32, align_bytes=64)
+            h2_scales = work.tile([P, COLS], U8, align_bytes=64)
+            for piece in range(pieces_of(r)):
+                cols = piece_cols(r, piece)
+                nc.vector.quantize_mx(
+                    out=h2_codes[:, cols].bitcast(FP8X4),
+                    scales=h2_scales[:, cols],
+                    in_=h2_grouped[:, cols, :].rearrange("p c t -> p (c t)"),
+                )
+            h2_q[r] = (h2_codes, h2_scales)
+
+        def layer2(r):
+            h2_codes, h2_scales = h2_q[r]
+            for tile_i in range(TILES):
+                slot = r * SLOTS_PER_ROUND + tile_i % SLOTS_PER_ROUND
+                nc.tensor.matmul_mx(
+                    out=acc[tile_i // SLOTS_PER_ROUND][:],
+                    lhsT=h2_codes[:, tile_i * P : (tile_i + 1) * P].bitcast(FP8X4),
+                    lhsT_scale=h2_scales[:, tile_i * P : (tile_i + 1) * P],
+                    rhs=w3_codes[:].bitcast(FP8X4),
+                    rhs_scale=w3_scales[:],
+                    start=(slot == 0),
+                    stop=(slot == SLOTS - 1),
+                )
 
         build_diags(0)
+        prepare_w2()
         build_diags(1)
         transpose_h1(0)
-        prepare_w2()
         for step in range(ROUNDS + LAG_LAYER2):
+            late = step - LAG_REGROUP
             if step < ROUNDS:
                 h1_grouped = group_h1(step)
-            if step >= LAG_LAYER2:
-                h2_grouped = regroup_h2(step - LAG_LAYER2)
+            if 0 <= late < ROUNDS:
+                h2_grouped = work.tile([P, COLS, PACK], BF16, align_bytes=64)
+                for piece in range(pieces_of(late)):
+                    regroup_h2(late, h2_grouped, piece)
             if 0 <= step - LAG_LAYER1 < ROUNDS:
                 layer1(step - LAG_LAYER1)
             if step < ROUNDS:
-                h1_q[step] = quantise(h1_grouped, "h1")
+                quantise_h1(step, h1_grouped)
             if step + 1 < ROUNDS:
                 transpose_h1(step + 1)
             if step >= LAG_LAYER2:
-                h2_codes, h2_scales = quantise(h2_grouped, "h2")
-                layer2(step - LAG_LAYER2, h2_codes, h2_scales)
+                layer2(step - LAG_LAYER2)
+            if 0 <= late < ROUNDS:
+                quantise_h2(late, h2_grouped)
             if step + 2 < ROUNDS:
                 build_diags(step + 2)
             if step == STEP_OF_W3:

@@ -27,7 +27,6 @@ LAG_REGROUP = 2
 LAG_LAYER2 = 3
 STEP_OF_W3 = 0
 STEP_OF_BASE = ROUNDS - 1
-LAST_ROUND_PIECES = NODE_BLOCKS
 
 FLOPS = 2 * 2 * (NODE_BLOCKS * P * SLOTS) * HID * HID
 
@@ -124,13 +123,6 @@ def tile_mpnnlayer_pb_kernel(tc, h1, h_V, mask_attend, W2, b2, W3, b3, out):
             nc.vector.quantize_mx(out=h1_codes[:].bitcast(FP8X4), scales=h1_scales[:], in_=h1_grouped[:])
             h1_q[r] = (h1_codes, h1_scales)
 
-        def pieces_of(r):
-            return LAST_ROUND_PIECES if r == ROUNDS - 1 else 1
-
-        def piece_cols(r, piece):
-            width = COLS // pieces_of(r)
-            return slice(piece * width, (piece + 1) * width)
-
         w2_codes = keep.tile([P, HID], U32, align_bytes=64)
         w2_scales = keep.tile([P, HID], U8, align_bytes=64)
         b2_f = keep.tile([P, PACK], F32)
@@ -149,30 +141,27 @@ def tile_mpnnlayer_pb_kernel(tc, h1, h_V, mask_attend, W2, b2, W3, b3, out):
         def layer1(r):
             codes, scales = h1_q[r]
             hidden = work.tile([P, PACK, COLS], BF16)
-            x_banks = [psum.tile([P, COLS], F32, name="x%d" % t2) for t2 in range(PACK)]
-            for piece in range(pieces_of(r)):
-                cols = piece_cols(r, piece)
-                for t2 in range(PACK):
-                    nc.tensor.matmul_mx(
-                        out=x_banks[t2][:, cols],
-                        lhsT=w2_codes[:, t2 * P : (t2 + 1) * P].bitcast(FP8X4),
-                        lhsT_scale=w2_scales[:, t2 * P : (t2 + 1) * P],
-                        rhs=codes[:, cols].bitcast(FP8X4),
-                        rhs_scale=scales[:, cols],
-                        start=True,
-                        stop=True,
-                    )
-                    nc.scalar.activation(
-                        out=hidden[:, t2, cols], in_=x_banks[t2][:, cols], func=ACT.Relu, bias=b2_f[:, t2 : t2 + 1], scale=1.0
-                    )
+            for t2 in range(PACK):
+                x_ps = psum.tile([P, COLS], F32, name="x%d" % t2)
+                nc.tensor.matmul_mx(
+                    out=x_ps[:],
+                    lhsT=w2_codes[:, t2 * P : (t2 + 1) * P].bitcast(FP8X4),
+                    lhsT_scale=w2_scales[:, t2 * P : (t2 + 1) * P],
+                    rhs=codes[:].bitcast(FP8X4),
+                    rhs_scale=scales[:],
+                    start=True,
+                    stop=True,
+                )
+                nc.scalar.activation(out=hidden[:, t2, :], in_=x_ps[:], func=ACT.Relu, bias=b2_f[:, t2 : t2 + 1], scale=1.0)
             hiddens[r] = hidden
 
-        def regroup_h2(r, h2_grouped, piece):
-            cols = piece_cols(r, piece)
+        def regroup_h2(r):
+            h2_grouped = work.tile([P, COLS, PACK], BF16, align_bytes=64)
             nc.vector.tensor_copy(
-                out=h2_grouped[:, cols, :].rearrange("p (c i) t -> p c t i", i=4),
-                in_=hiddens[r][:, :, cols].rearrange("p t (c i) -> p c t i", i=4),
+                out=h2_grouped[:].rearrange("p (c i) t -> p c t i", i=4),
+                in_=hiddens[r][:].rearrange("p t (c i) -> p c t i", i=4),
             )
+            return h2_grouped
 
         w3_codes = keep.tile([P, HID], U32, align_bytes=64)
         w3_scales = keep.tile([P, HID], U8, align_bytes=64)
@@ -234,13 +223,9 @@ def tile_mpnnlayer_pb_kernel(tc, h1, h_V, mask_attend, W2, b2, W3, b3, out):
         def quantise_h2(r, h2_grouped):
             h2_codes = work.tile([P, COLS], U32, align_bytes=64)
             h2_scales = work.tile([P, COLS], U8, align_bytes=64)
-            for piece in range(pieces_of(r)):
-                cols = piece_cols(r, piece)
-                nc.vector.quantize_mx(
-                    out=h2_codes[:, cols].bitcast(FP8X4),
-                    scales=h2_scales[:, cols],
-                    in_=h2_grouped[:, cols, :].rearrange("p c t -> p (c t)"),
-                )
+            nc.vector.quantize_mx(
+                out=h2_codes[:].bitcast(FP8X4), scales=h2_scales[:], in_=h2_grouped[:].rearrange("p c t -> p (c t)")
+            )
             h2_q[r] = (h2_codes, h2_scales)
 
         def layer2(r):
@@ -266,9 +251,7 @@ def tile_mpnnlayer_pb_kernel(tc, h1, h_V, mask_attend, W2, b2, W3, b3, out):
             if step < ROUNDS:
                 h1_grouped = group_h1(step)
             if 0 <= late < ROUNDS:
-                h2_grouped = work.tile([P, COLS, PACK], BF16, align_bytes=64)
-                for piece in range(pieces_of(late)):
-                    regroup_h2(late, h2_grouped, piece)
+                h2_grouped = regroup_h2(late)
             if 0 <= step - LAG_LAYER1 < ROUNDS:
                 layer1(step - LAG_LAYER1)
             if step < ROUNDS:

@@ -26,6 +26,7 @@ LAG_LAYER1 = 1
 LAG_REGROUP = 2
 LAG_LAYER2 = 3
 STEP_OF_W3 = 0
+STEP_OF_SHARES = ROUNDS - 2
 STEP_OF_BASE = ROUNDS - 1
 
 FLOPS = 2 * 2 * (NODE_BLOCKS * P * SLOTS) * HID * HID
@@ -107,21 +108,23 @@ def tile_mpnnlayer_pb_kernel(tc, h1, h_V, mask_attend, W2, b2, W3, b3, out):
                         )
                 banks[r].append(bank)
 
-        def group_h1(r):
-            h1_grouped = work.tile([P, COLS * PACK], BF16, align_bytes=64)
-            grouped_words = h1_grouped[:].bitcast(F32).rearrange("p (c u) -> p c u", u=2)
+        def group_h1(r, grouped):
+            grouped_words = grouped[:, 0, :].bitcast(F32).rearrange("p (c u) -> p c u", u=2)
             for nb in range(NODE_BLOCKS):
                 nc.scalar.copy(
                     out=grouped_words[:, nb * SLOTS_PER_ROUND * P : (nb + 1) * SLOTS_PER_ROUND * P, :],
                     in_=banks[r][nb][:].rearrange("p u c -> p c u"),
                 )
-            return h1_grouped
 
-        def quantise_h1(r, h1_grouped):
-            h1_codes = work.tile([P, COLS], U32, align_bytes=64)
-            h1_scales = work.tile([P, COLS], U8, align_bytes=64)
-            nc.vector.quantize_mx(out=h1_codes[:].bitcast(FP8X4), scales=h1_scales[:], in_=h1_grouped[:])
-            h1_q[r] = (h1_codes, h1_scales)
+        def quantise(grouped, first, last):
+            codes = work.tile([P, 2, COLS], U32, align_bytes=64)
+            scales = work.tile([P, 2, COLS], U8, align_bytes=64)
+            nc.vector.quantize_mx(
+                out=codes[:, first:last, :].rearrange("p h c -> p (h c)").bitcast(FP8X4),
+                scales=scales[:, first:last, :].rearrange("p h c -> p (h c)"),
+                in_=grouped[:, first:last, :].rearrange("p h c -> p (h c)"),
+            )
+            return codes, scales
 
         w2_codes = keep.tile([P, HID], U32, align_bytes=64)
         w2_scales = keep.tile([P, HID], U8, align_bytes=64)
@@ -147,21 +150,19 @@ def tile_mpnnlayer_pb_kernel(tc, h1, h_V, mask_attend, W2, b2, W3, b3, out):
                     out=x_ps[:],
                     lhsT=w2_codes[:, t2 * P : (t2 + 1) * P].bitcast(FP8X4),
                     lhsT_scale=w2_scales[:, t2 * P : (t2 + 1) * P],
-                    rhs=codes[:].bitcast(FP8X4),
-                    rhs_scale=scales[:],
+                    rhs=codes[:, 0, :].bitcast(FP8X4),
+                    rhs_scale=scales[:, 0, :],
                     start=True,
                     stop=True,
                 )
                 nc.scalar.activation(out=hidden[:, t2, :], in_=x_ps[:], func=ACT.Relu, bias=b2_f[:, t2 : t2 + 1], scale=1.0)
             hiddens[r] = hidden
 
-        def regroup_h2(r):
-            h2_grouped = work.tile([P, COLS, PACK], BF16, align_bytes=64)
+        def regroup_h2(r, grouped):
             nc.vector.tensor_copy(
-                out=h2_grouped[:].rearrange("p (c i) t -> p c t i", i=4),
+                out=grouped[:, 1, :].rearrange("p (c i t) -> p c t i", i=4, t=PACK),
                 in_=hiddens[r][:].rearrange("p t (c i) -> p c t i", i=4),
             )
-            return h2_grouped
 
         w3_codes = keep.tile([P, HID], U32, align_bytes=64)
         w3_scales = keep.tile([P, HID], U8, align_bytes=64)
@@ -175,7 +176,11 @@ def tile_mpnnlayer_pb_kernel(tc, h1, h_V, mask_attend, W2, b2, W3, b3, out):
 
         base = keep.tile([P, NODE_BLOCKS, HID], F32)
 
-        def prepare_base():
+        idle_codes = keep.tile([P, P], U32, align_bytes=64)
+        idle_scales = keep.tile([P, P], U8, align_bytes=64)
+        minus_masked_share = keep.tile([P, NODE_BLOCKS], F32)
+
+        def prepare_shares():
             idle_grouped = keep.tile([P, P, PACK], BF16, align_bytes=64)
             nc.vector.tensor_scalar(
                 out=idle_grouped[:],
@@ -186,11 +191,21 @@ def tile_mpnnlayer_pb_kernel(tc, h1, h_V, mask_attend, W2, b2, W3, b3, out):
             )
             count = keep.tile([P, NODE_BLOCKS], F32)
             nc.vector.reduce_sum(out=count[:], in_=mask_f[:].rearrange("q r nb s -> q nb r s"), axis=mybir.AxisListType.XY)
-            idle_codes = keep.tile([P, P], U32, align_bytes=64)
-            idle_scales = keep.tile([P, P], U8, align_bytes=64)
             nc.vector.quantize_mx(
                 out=idle_codes[:].bitcast(FP8X4), scales=idle_scales[:], in_=idle_grouped[:].rearrange("p c t -> p (c t)")
             )
+            kept_share = keep.tile([P, NODE_BLOCKS], F32)
+            nc.vector.tensor_scalar(out=kept_share[:], in0=count[:], scalar1=1.0 / SLOTS, scalar2=None, op0=ALU.mult)
+            nc.vector.tensor_scalar(
+                out=minus_masked_share[:], in0=count[:], scalar1=1.0 / SLOTS, scalar2=-1.0, op0=ALU.mult, op1=ALU.add
+            )
+            for nb in range(NODE_BLOCKS):
+                nc.vector.scalar_tensor_tensor(
+                    out=base[:, nb, :], in0=b3_all[:], scalar=kept_share[:, nb : nb + 1], in1=hv[:, nb, :],
+                    op0=ALU.mult, op1=ALU.add,
+                )
+
+        def prepare_base():
             idle_ps = psum.tile([P, HID], F32, name="xt0")
             nc.tensor.matmul_mx(
                 out=idle_ps[:],
@@ -201,17 +216,6 @@ def tile_mpnnlayer_pb_kernel(tc, h1, h_V, mask_attend, W2, b2, W3, b3, out):
                 start=True,
                 stop=True,
             )
-            kept_share = keep.tile([P, NODE_BLOCKS], F32)
-            nc.vector.tensor_scalar(out=kept_share[:], in0=count[:], scalar1=1.0 / SLOTS, scalar2=None, op0=ALU.mult)
-            minus_masked_share = keep.tile([P, NODE_BLOCKS], F32)
-            nc.vector.tensor_scalar(
-                out=minus_masked_share[:], in0=count[:], scalar1=1.0 / SLOTS, scalar2=-1.0, op0=ALU.mult, op1=ALU.add
-            )
-            for nb in range(NODE_BLOCKS):
-                nc.vector.scalar_tensor_tensor(
-                    out=base[:, nb, :], in0=b3_all[:], scalar=kept_share[:, nb : nb + 1], in1=hv[:, nb, :],
-                    op0=ALU.mult, op1=ALU.add,
-                )
             for nb in range(NODE_BLOCKS):
                 nc.vector.scalar_tensor_tensor(
                     out=base[:, nb, :], in0=idle_ps[:], scalar=minus_masked_share[:, nb : nb + 1], in1=base[:, nb, :],
@@ -220,22 +224,14 @@ def tile_mpnnlayer_pb_kernel(tc, h1, h_V, mask_attend, W2, b2, W3, b3, out):
 
         acc = [psum.tile([P, HID], F32, name="acc%d" % nb) for nb in range(NODE_BLOCKS)]
 
-        def quantise_h2(r, h2_grouped):
-            h2_codes = work.tile([P, COLS], U32, align_bytes=64)
-            h2_scales = work.tile([P, COLS], U8, align_bytes=64)
-            nc.vector.quantize_mx(
-                out=h2_codes[:].bitcast(FP8X4), scales=h2_scales[:], in_=h2_grouped[:].rearrange("p c t -> p (c t)")
-            )
-            h2_q[r] = (h2_codes, h2_scales)
-
         def layer2(r):
-            h2_codes, h2_scales = h2_q[r]
+            codes, scales = h2_q[r]
             for tile_i in range(TILES):
                 slot = r * SLOTS_PER_ROUND + tile_i % SLOTS_PER_ROUND
                 nc.tensor.matmul_mx(
                     out=acc[tile_i // SLOTS_PER_ROUND][:],
-                    lhsT=h2_codes[:, tile_i * P : (tile_i + 1) * P].bitcast(FP8X4),
-                    lhsT_scale=h2_scales[:, tile_i * P : (tile_i + 1) * P],
+                    lhsT=codes[:, 1, tile_i * P : (tile_i + 1) * P].bitcast(FP8X4),
+                    lhsT_scale=scales[:, 1, tile_i * P : (tile_i + 1) * P],
                     rhs=w3_codes[:].bitcast(FP8X4),
                     rhs_scale=w3_scales[:],
                     start=(slot == 0),
@@ -248,24 +244,32 @@ def tile_mpnnlayer_pb_kernel(tc, h1, h_V, mask_attend, W2, b2, W3, b3, out):
         transpose_h1(0)
         for step in range(ROUNDS + LAG_LAYER2):
             late = step - LAG_REGROUP
-            if step < ROUNDS:
-                h1_grouped = group_h1(step)
-            if 0 <= late < ROUNDS:
-                h2_grouped = regroup_h2(late)
+            has_h1 = step < ROUNDS
+            has_h2 = 0 <= late < ROUNDS
+            if has_h1 or has_h2:
+                grouped = work.tile([P, 2, COLS * PACK], BF16, align_bytes=64)
+            if has_h1:
+                group_h1(step, grouped)
+            if has_h2:
+                regroup_h2(late, grouped)
             if 0 <= step - LAG_LAYER1 < ROUNDS:
                 layer1(step - LAG_LAYER1)
-            if step < ROUNDS:
-                quantise_h1(step, h1_grouped)
+            if step + 2 < ROUNDS:
+                build_diags(step + 2)
             if step + 1 < ROUNDS:
                 transpose_h1(step + 1)
             if step >= LAG_LAYER2:
                 layer2(step - LAG_LAYER2)
-            if 0 <= late < ROUNDS:
-                quantise_h2(late, h2_grouped)
-            if step + 2 < ROUNDS:
-                build_diags(step + 2)
+            if has_h1 or has_h2:
+                quantised = quantise(grouped, 0 if has_h1 else 1, 2 if has_h2 else 1)
+            if has_h1:
+                h1_q[step] = quantised
+            if has_h2:
+                h2_q[late] = quantised
             if step == STEP_OF_W3:
                 prepare_w3()
+            if step == STEP_OF_SHARES:
+                prepare_shares()
             if step == STEP_OF_BASE:
                 prepare_base()
 

from contextlib import ExitStack

import concourse.mybir as mybir
from concourse.masks import make_identity

F32 = mybir.dt.float32
BF16 = mybir.dt.bfloat16
U32 = mybir.dt.uint32
U8 = mybir.dt.uint8
FP8X4 = mybir.dt.float8_e4m3fn_x4
ALU = mybir.AluOpType
ACT = mybir.ActivationFunctionType

P = 128
PACK = 4
HID = 512
WORDS = HID // 2
SLOTS = 30
NODE_BLOCKS = 2
SLOTS_PER_ROUND = 2
TILES = NODE_BLOCKS * SLOTS_PER_ROUND
COLS = TILES * P
ROUNDS = SLOTS // SLOTS_PER_ROUND

LAG_LAYER1 = 1
LAG_REGROUP = 2
LAG_LAYER2 = 3
STEP_OF_W3 = 0
STEP_OF_SHARES = ROUNDS - 2
STEP_OF_BASE = ROUNDS - 1

FLOPS = 2 * 2 * (NODE_BLOCKS * P * SLOTS) * HID * HID


def tile_mpnnlayer_pb_kernel(tc, h1, h_V, mask_attend, W2, b2, W3, b3, out):
    nc = tc.nc
    h1_rows = h1.rearrange("b n k h -> (b n) (k h)")
    hv_rows = h_V.rearrange("b n h -> (b n) h")
    mask_rows = mask_attend.rearrange("b n k -> (b n) k")
    out_rows = out.rearrange("b n h -> (b n) h")

    with ExitStack() as ctx:
        ctx.enter_context(tc.manual_schedule())
        keep = ctx.enter_context(tc.tile_pool(name="keep", bufs=1))
        work = ctx.enter_context(tc.tile_pool(name="work", bufs=3))
        psum = ctx.enter_context(tc.psum_pool(name="psum", bufs=1))

        h1_sb = [keep.tile([P, SLOTS * HID], BF16, name="h1_sb%d" % nb) for nb in range(NODE_BLOCKS)]

        def load_h1(r):
            cols = slice(r * SLOTS_PER_ROUND * HID, (r + 1) * SLOTS_PER_ROUND * HID)
            for nb in range(NODE_BLOCKS):
                nc.sync.dma_start(out=h1_sb[nb][:, cols], in_=h1_rows[nb * P : (nb + 1) * P, cols])

        mask_bf = keep.tile([P, NODE_BLOCKS, SLOTS], BF16)
        nc.sync.dma_start(out=mask_bf[:], in_=mask_rows.rearrange("(nb q) k -> q nb k", q=P))
        w2_raw = keep.tile([P, PACK, HID], BF16)
        for u in range(2):
            nc.sync.dma_start(
                out=w2_raw[:, 2 * u : 2 * u + 2, :],
                in_=W2[u * 2 * P : (u + 1) * 2 * P, :].rearrange("(p e) f -> p e f", e=2),
            )
        b2_bf = keep.tile([P, PACK], BF16)
        nc.sync.dma_start(out=b2_bf[:], in_=b2.rearrange("(p t) -> p t", t=PACK))
        load_h1(0)
        load_h1(1)
        w3_raw = keep.tile([P, PACK, HID], BF16)
        nc.sync.dma_start(out=w3_raw[:], in_=W3.rearrange("(p t) f -> p t f", t=PACK))
        for r in range(2, ROUNDS):
            load_h1(r)
        b3_all = keep.tile([P, HID], BF16)
        nc.sync.dma_start(out=b3_all[:], in_=b3.partition_broadcast(P))
        hv = keep.tile([P, NODE_BLOCKS, HID], BF16)
        nc.sync.dma_start(out=hv[:], in_=hv_rows.rearrange("(nb q) h -> q nb h", q=P))

        ident = keep.tile([P, P], F32)
        make_identity(nc, ident[:])
        mask_f = keep.tile([P, ROUNDS, NODE_BLOCKS, SLOTS_PER_ROUND], F32)
        nc.vector.tensor_copy(out=mask_f[:], in_=mask_bf[:].rearrange("q nb (r s) -> q r nb s", s=SLOTS_PER_ROUND))
        h1_words = [h1_sb[nb][:].bitcast(F32) for nb in range(NODE_BLOCKS)]
        diags = {}
        banks = {}
        h1_q = {}
        hiddens = {}
        h2_q = {}

        def build_diags(r):
            diag = work.tile([P, TILES, P], F32)
            nc.vector.tensor_tensor(
                out=diag[:],
                in0=ident[:].unsqueeze(1).to_broadcast([P, TILES, P]),
                in1=mask_f[:, r, :, :].rearrange("q nb s -> q (nb s)").unsqueeze(2).to_broadcast([P, TILES, P]),
                op=ALU.mult,
            )
            diags[r] = diag

        def transpose_h1(r):
            banks[r] = []
            for nb in range(NODE_BLOCKS):
                bank = psum.tile([P, 2, SLOTS_PER_ROUND * P], F32, name="xt%d" % nb)
                for s in range(SLOTS_PER_ROUND):
                    for u in range(2):
                        first = (r * SLOTS_PER_ROUND + s) * WORDS + u * P
                        nc.tensor.transpose(
                            bank[:, u, s * P : (s + 1) * P],
                            h1_words[nb][:, first : first + P],
                            diags[r][:, nb * SLOTS_PER_ROUND + s, :],
                        )
                banks[r].append(bank)

        def group_h1(r, grouped):
            grouped_words = grouped[:, 0, :].bitcast(F32).rearrange("p (c u) -> p c u", u=2)
            for nb in range(NODE_BLOCKS):
                nc.scalar.copy(
                    out=grouped_words[:, nb * SLOTS_PER_ROUND * P : (nb + 1) * SLOTS_PER_ROUND * P, :],
                    in_=banks[r][nb][:].rearrange("p u c -> p c u"),
                )

        def quantise(grouped, first, last):
            codes = work.tile([P, 2, COLS], U32, align_bytes=64)
            scales = work.tile([P, 2, COLS], U8, align_bytes=64)
            nc.vector.quantize_mx(
                out=codes[:, first:last, :].rearrange("p h c -> p (h c)").bitcast(FP8X4),
                scales=scales[:, first:last, :].rearrange("p h c -> p (h c)"),
                in_=grouped[:, first:last, :].rearrange("p h c -> p (h c)"),
            )
            return codes, scales

        w2_codes = keep.tile([P, HID], U32, align_bytes=64)
        w2_scales = keep.tile([P, HID], U8, align_bytes=64)
        b2_f = keep.tile([P, PACK], F32)

        def prepare_w2():
            nc.vector.tensor_copy(out=b2_f[:], in_=b2_bf[:])
            w2_grouped = keep.tile([P, HID, PACK], BF16, align_bytes=64)
            nc.vector.tensor_copy(
                out=w2_grouped[:].rearrange("p (t2 c) t -> p t2 c t", t2=PACK),
                in_=w2_raw[:].rearrange("p t (c t2) -> p t2 c t", t2=PACK),
            )
            nc.vector.quantize_mx(
                out=w2_codes[:].bitcast(FP8X4), scales=w2_scales[:], in_=w2_grouped[:].rearrange("p c t -> p (c t)")
            )

        def layer1(r):
            codes, scales = h1_q[r]
            hidden = work.tile([P, PACK, COLS], BF16)
            for t2 in range(PACK):
                x_ps = psum.tile([P, COLS], F32, name="x%d" % t2)
                nc.tensor.matmul_mx(
                    out=x_ps[:],
                    lhsT=w2_codes[:, t2 * P : (t2 + 1) * P].bitcast(FP8X4),
                    lhsT_scale=w2_scales[:, t2 * P : (t2 + 1) * P],
                    rhs=codes[:, 0, :].bitcast(FP8X4),
                    rhs_scale=scales[:, 0, :],
                    start=True,
                    stop=True,
                )
                nc.scalar.activation(out=hidden[:, t2, :], in_=x_ps[:], func=ACT.Relu, bias=b2_f[:, t2 : t2 + 1], scale=1.0)
            hiddens[r] = hidden

        def regroup_h2(r, grouped):
            nc.vector.tensor_copy(
                out=grouped[:, 1, :].rearrange("p (c i t) -> p c t i", i=4, t=PACK),
                in_=hiddens[r][:].rearrange("p t (c i) -> p c t i", i=4),
            )

        w3_codes = keep.tile([P, HID], U32, align_bytes=64)
        w3_scales = keep.tile([P, HID], U8, align_bytes=64)

        def prepare_w3():
            w3_grouped = keep.tile([P, HID, PACK], BF16, align_bytes=64)
            nc.vector.tensor_copy(out=w3_grouped[:], in_=w3_raw[:].rearrange("p t f -> p f t"))
            nc.vector.quantize_mx(
                out=w3_codes[:].bitcast(FP8X4), scales=w3_scales[:], in_=w3_grouped[:].rearrange("p f t -> p (f t)")
            )

        base = keep.tile([P, NODE_BLOCKS, HID], F32)

        idle_codes = keep.tile([P, P], U32, align_bytes=64)
        idle_scales = keep.tile([P, P], U8, align_bytes=64)
        minus_masked_share = keep.tile([P, NODE_BLOCKS], F32)

        def prepare_shares():
            idle_grouped = keep.tile([P, P, PACK], BF16, align_bytes=64)
            nc.vector.tensor_scalar(
                out=idle_grouped[:],
                in0=b2_f[:].unsqueeze(1).to_broadcast([P, P, PACK]),
                scalar1=0.0,
                scalar2=None,
                op0=ALU.max,
            )
            count = keep.tile([P, NODE_BLOCKS], F32)
            nc.vector.reduce_sum(out=count[:], in_=mask_f[:].rearrange("q r nb s -> q nb r s"), axis=mybir.AxisListType.XY)
            nc.vector.quantize_mx(
                out=idle_codes[:].bitcast(FP8X4), scales=idle_scales[:], in_=idle_grouped[:].rearrange("p c t -> p (c t)")
            )
            kept_share = keep.tile([P, NODE_BLOCKS], F32)
            nc.vector.tensor_scalar(out=kept_share[:], in0=count[:], scalar1=1.0 / SLOTS, scalar2=None, op0=ALU.mult)
            nc.vector.tensor_scalar(
                out=minus_masked_share[:], in0=count[:], scalar1=1.0 / SLOTS, scalar2=-1.0, op0=ALU.mult, op1=ALU.add
            )
            for nb in range(NODE_BLOCKS):
                nc.vector.scalar_tensor_tensor(
                    out=base[:, nb, :], in0=b3_all[:], scalar=kept_share[:, nb : nb + 1], in1=hv[:, nb, :],
                    op0=ALU.mult, op1=ALU.add,
                )

        def prepare_base():
            idle_ps = psum.tile([P, HID], F32, name="xt0")
            nc.tensor.matmul_mx(
                out=idle_ps[:],
                lhsT=idle_codes[:].bitcast(FP8X4),
                lhsT_scale=idle_scales[:],
                rhs=w3_codes[:].bitcast(FP8X4),
                rhs_scale=w3_scales[:],
                start=True,
                stop=True,
            )
            for nb in range(NODE_BLOCKS):
                nc.vector.scalar_tensor_tensor(
                    out=base[:, nb, :], in0=idle_ps[:], scalar=minus_masked_share[:, nb : nb + 1], in1=base[:, nb, :],
                    op0=ALU.mult, op1=ALU.add,
                )

        acc = [psum.tile([P, HID], F32, name="acc%d" % nb) for nb in range(NODE_BLOCKS)]

        def layer2(r):
            codes, scales = h2_q[r]
            for tile_i in range(TILES):
                slot = r * SLOTS_PER_ROUND + tile_i % SLOTS_PER_ROUND
                nc.tensor.matmul_mx(
                    out=acc[tile_i // SLOTS_PER_ROUND][:],
                    lhsT=codes[:, 1, tile_i * P : (tile_i + 1) * P].bitcast(FP8X4),
                    lhsT_scale=scales[:, 1, tile_i * P : (tile_i + 1) * P],
                    rhs=w3_codes[:].bitcast(FP8X4),
                    rhs_scale=w3_scales[:],
                    start=(slot == 0),
                    stop=(slot == SLOTS - 1),
                )

        build_diags(0)
        prepare_w2()
        build_diags(1)
        transpose_h1(0)
        for step in range(ROUNDS + LAG_LAYER2):
            late = step - LAG_REGROUP
            has_h1 = step < ROUNDS
            has_h2 = 0 <= late < ROUNDS
            if has_h1 or has_h2:
                grouped = work.tile([P, 2, COLS * PACK], BF16, align_bytes=64)
            if has_h1:
                group_h1(step, grouped)
            if has_h2:
                regroup_h2(late, grouped)
            if 0 <= step - LAG_LAYER1 < ROUNDS:
                layer1(step - LAG_LAYER1)
            if step + 2 < ROUNDS:
                build_diags(step + 2)
            if step + 1 < ROUNDS:
                transpose_h1(step + 1)
            if step >= LAG_LAYER2:
                layer2(step - LAG_LAYER2)
            if has_h1 or has_h2:
                quantised = quantise(grouped, 0 if has_h1 else 1, 2 if has_h2 else 1)
            if has_h1:
                h1_q[step] = quantised
            if has_h2:
                h2_q[late] = quantised
            if step == STEP_OF_W3:
                prepare_w3()
            if step == STEP_OF_SHARES:
                prepare_shares()
            if step == STEP_OF_BASE:
                prepare_base()

        result = keep.tile([P, NODE_BLOCKS, HID], F32)
        for nb in range(NODE_BLOCKS):
            nc.vector.scalar_tensor_tensor(
                out=result[:, nb, :], in0=acc[nb][:], scalar=1.0 / SLOTS, in1=base[:, nb, :], op0=ALU.mult, op1=ALU.add
            )
            nc.sync.dma_start(out=out_rows[nb * P : (nb + 1) * P, :], in_=result[:, nb, :])
